import numpy as np
import ml_dtypes


def mxq(x, axis, fmt="e4m3"):
    dtype, down = {"e4m3": (ml_dtypes.float8_e4m3fn, 7), "e5m2": (ml_dtypes.float8_e5m2, 14)}[fmt]
    v = np.moveaxis(np.asarray(x, np.float32).astype(ml_dtypes.bfloat16).astype(np.float64), axis, -1)
    blocks = v.reshape(v.shape[:-1] + (-1, 32))
    amax = np.abs(blocks).max(-1, keepdims=True)
    byte = np.maximum(np.where(amax > 0, np.frexp(amax)[1] - 1 + 127, 0) - down, 1)
    scale = np.exp2(byte - 127.0)
    codes = (blocks / scale).astype(np.float32).astype(dtype).astype(np.float64)
    return np.moveaxis((codes * scale).reshape(v.shape), -1, axis)


WIDE = False


def mx_kscale(k):
    if not WIDE:
        return np.ones(k)
    levels = np.array([10, -10, 5, -5, 0])
    a = np.random.permutation(np.resize(levels, k // 512 * 4)).reshape(k // 512, 4)
    idx = np.arange(k)
    return np.exp2(a[idx // 512, idx % 128 // 32])


BF16 = ml_dtypes.bfloat16


def bf(x):
    return np.asarray(x, np.float32).astype(BF16)


def f64(x):
    return np.asarray(x).astype(np.float64)


B, C, H, W = 8, 512, 16, 16
HW = H * W
N = B * HW


def setup_inputs():
    s = mx_kscale(C)
    return {"x": bf(np.random.standard_normal((B, C, H, W)) * s[None, :, None, None]),
            "w_g": bf(np.random.standard_normal((C, C)) * 0.5 / np.sqrt(C) / s[None, :])}


def reference(x, w_g):
    xf = f64(x).reshape(B, C, HW).transpose(0, 2, 1)
    g = mxq(xf, 2, "e4m3") @ mxq(f64(w_g), 1, "e4m3").T
    gq = mxq(g, 2, "e4m3").reshape(N, C)
    p = (gq @ gq.T).reshape(B, HW, B, HW)
    gmax = p.max(axis=2)
    return gmax.transpose(1, 0, 2)

@@ -1,0 +1,156 @@
+from contextlib import ExitStack
+
+import concourse.mybir as mybir
+from concourse.masks import make_identity
+
+F32 = mybir.dt.float32
+BF16 = mybir.dt.bfloat16
+U32 = mybir.dt.uint32
+U8 = mybir.dt.uint8
+FP8X4 = mybir.dt.float8_e4m3fn_x4
+
+P = 128
+PACK = 4
+IMAGES = 8
+CHANNELS = 512
+PIXELS = 256
+HALVES = PIXELS // P
+PAIR = 2
+
+FLOPS = 2 * IMAGES * PIXELS * CHANNELS * (CHANNELS + IMAGES * PIXELS)
+
+STAGE1_BANKS = 3
+STAGE2_BANKS = 5
+RUN = 4
+VECTOR_REGROUPS = 6
+X_AHEAD = 3
+G_AHEAD = 2
+
+
+def tile_nlgp_pa_kernel(tc, x, w_g, out):
+    nc = tc.nc
+    with ExitStack() as ctx:
+        keep = ctx.enter_context(tc.tile_pool(name="keep", bufs=1))
+        psum_stage1 = ctx.enter_context(tc.psum_pool(name="psum_stage1", bufs=STAGE1_BANKS))
+        psum_stage2 = ctx.enter_context(tc.psum_pool(name="psum_stage2", bufs=STAGE2_BANKS))
+        ctx.enter_context(tc.manual_schedule())
+
+        images = range(IMAGES)
+        x_raw = [keep.tile([P, PACK, PIXELS], BF16, name="x_raw%d" % b) for b in images]
+        x_grouped = [keep.tile([P, PIXELS, PACK], BF16, name="x_grouped%d" % b, align_bytes=64) for b in images]
+        x_codes = [keep.tile([P, PIXELS], U32, name="x_codes%d" % b, align_bytes=64) for b in images]
+        x_scales = [keep.tile([P, PIXELS], U8, name="x_scales%d" % b, align_bytes=64) for b in images]
+        g_grouped = [keep.tile([P, PIXELS, PACK], BF16, name="g_grouped%d" % b, align_bytes=64) for b in images]
+        g_codes = [keep.tile([P, PIXELS], U32, name="g_codes%d" % b, align_bytes=64) for b in images]
+        g_scales = [keep.tile([P, PIXELS], U8, name="g_scales%d" % b, align_bytes=64) for b in images]
+        best = [keep.tile([P, HALVES, PIXELS], F32, name="best%d" % b) for b in images]
+        w_raw = keep.tile([P, PACK * CHANNELS], BF16, name="w_raw")
+        w_grouped = keep.tile([P, CHANNELS * PACK], BF16, name="w_grouped", align_bytes=64)
+        w_codes = keep.tile([P, CHANNELS], U32, name="w_codes", align_bytes=64)
+        w_scales = keep.tile([P, CHANNELS], U8, name="w_scales", align_bytes=64)
+        identity = keep.tile([P, P], F32, name="identity")
+
+        nc.sync.dma_start(out=w_raw[:], in_=w_g.rearrange("(p t) c -> p (t c)", t=PACK))
+        for b in images:
+            nc.sync.dma_start(out=x_raw[b][:], in_=x[b].rearrange("(q t) h w -> q t (h w)", t=PACK))
+        make_identity(nc, identity[:])
+
+        def regroup_x(b):
+            source = x_raw[b][:].rearrange("q t (n i) -> q n t i", i=RUN)
+            target = x_grouped[b][:].rearrange("q (n i) t -> q n t i", i=RUN)
+            if b < VECTOR_REGROUPS:
+                nc.vector.tensor_copy(out=target, in_=source)
+            else:
+                nc.scalar.copy(out=target, in_=source)
+
+        def quantise_x(b):
+            nc.vector.quantize_mx(
+                out=x_codes[b][:].bitcast(FP8X4),
+                scales=x_scales[b][:],
+                in_=x_grouped[b][:].rearrange("q i t -> q (i t)"),
+            )
+
+        def quantise_w():
+            w_words = w_raw[:].bitcast(F32).rearrange("p (t q u) -> p t u q", t=PACK, u=PAIR)
+            grouped_words = w_grouped[:].bitcast(F32).rearrange("q (t p u) -> q t p u", t=PACK, u=PAIR)
+            for first_t in range(0, PACK, 2):
+                w_bank = psum_stage1.tile([P, 2, PAIR, P], F32, tag="bank")
+                for t in range(2):
+                    for u in range(PAIR):
+                        nc.tensor.transpose(w_bank[:, t, u, :], w_words[:, first_t + t, u, :], identity[:])
+                target = grouped_words[:, first_t : first_t + 2, :, :]
+                source = w_bank[:].rearrange("q t u p -> q t p u")
+                if first_t == 0:
+                    nc.scalar.copy(out=target, in_=source)
+                else:
+                    nc.vector.tensor_copy(out=target, in_=source)
+            nc.vector.quantize_mx(out=w_codes[:].bitcast(FP8X4), scales=w_scales[:], in_=w_grouped[:])
+
+        def project(b):
+            for h in range(HALVES):
+                pixels = slice(h * P, (h + 1) * P)
+                g_bank = psum_stage1.tile([P, PACK, P], F32, tag="bank")
+                for t in range(PACK):
+                    d_cols = slice(t * P, (t + 1) * P)
+                    nc.tensor.matmul_mx(
+                        out=g_bank[:, t, :],
+                        lhsT=w_codes[:, d_cols].bitcast(FP8X4),
+                        lhsT_scale=w_scales[:, d_cols],
+                        rhs=x_codes[b][:, pixels].bitcast(FP8X4),
+                        rhs_scale=x_scales[b][:, pixels],
+                        start=True,
+                        stop=True,
+                    )
+                nc.scalar.copy(out=g_grouped[b][:, pixels, :], in_=g_bank[:].rearrange("p t i -> p i t"))
+
+        def quantise_g(b):
+            nc.vector.quantize_mx(
+                out=g_codes[b][:].bitcast(FP8X4),
+                scales=g_scales[b][:],
+                in_=g_grouped[b][:].rearrange("p i t -> p (i t)"),
+            )
+
+        def gram_block(b1, b2):
+            p_bank = psum_stage2.tile([P, HALVES, PIXELS], F32, tag="bank")
+            for h in range(HALVES):
+                rows = slice(h * P, (h + 1) * P)
+                nc.tensor.matmul_mx(
+                    out=p_bank[:, h, :],
+                    lhsT=g_codes[b1][:, rows].bitcast(FP8X4),
+                    lhsT_scale=g_scales[b1][:, rows],
+                    rhs=g_codes[b2][:].bitcast(FP8X4),
+                    rhs_scale=g_scales[b2][:],
+                    start=True,
+                    stop=True,
+                )
+            if b2 == 0:
+                nc.scalar.copy(out=best[b1][:], in_=p_bank[:])
+            else:
+                nc.vector.tensor_tensor(out=best[b1][:], in0=p_bank[:], in1=best[b1][:], op=mybir.AluOpType.max)
+            if b2 == IMAGES - 1:
+                nc.sync.dma_start(out=out.rearrange("(h p) b j -> p h b j", p=P)[:, :, b1, :], in_=best[b1][:])
+
+        def gram_step(s):
+            for k in range(s):
+                gram_block(k, s)
+                gram_block(s, k)
+            gram_block(s, s)
+
+        regroup_x(0)
+        quantise_w()
+        for b in range(X_AHEAD):
+            regroup_x(b + 1)
+            quantise_x(b)
+        for b in range(G_AHEAD):
+            project(b)
+        quantise_g(0)
+        for s in images:
+            if s + X_AHEAD + 1 < IMAGES:
+                regroup_x(s + X_AHEAD + 1)
+            if s + X_AHEAD < IMAGES:
+                quantise_x(s + X_AHEAD)
+            if s + G_AHEAD < IMAGES:
+                project(s + G_AHEAD)
+            if s + 1 < IMAGES:
+                quantise_g(s + 1)
+            gram_step(s)

@@ -33,7 +33,6 @@ def tile_nlgp_pa_kernel(tc, x, w_g, out):
         keep = ctx.enter_context(tc.tile_pool(name="keep", bufs=1))
         psum_stage1 = ctx.enter_context(tc.psum_pool(name="psum_stage1", bufs=STAGE1_BANKS))
         psum_stage2 = ctx.enter_context(tc.psum_pool(name="psum_stage2", bufs=STAGE2_BANKS))
-        ctx.enter_context(tc.manual_schedule())
 
         images = range(IMAGES)
         x_raw = [keep.tile([P, PACK, PIXELS], BF16, name="x_raw%d" % b) for b in images]

@@ -33,6 +33,7 @@ def tile_nlgp_pa_kernel(tc, x, w_g, out):
         keep = ctx.enter_context(tc.tile_pool(name="keep", bufs=1))
         psum_stage1 = ctx.enter_context(tc.psum_pool(name="psum_stage1", bufs=STAGE1_BANKS))
         psum_stage2 = ctx.enter_context(tc.psum_pool(name="psum_stage2", bufs=STAGE2_BANKS))
+        ctx.enter_context(tc.manual_schedule())
 
         images = range(IMAGES)
         x_raw = [keep.tile([P, PACK, PIXELS], BF16, name="x_raw%d" % b) for b in images]
@@ -49,7 +50,12 @@ def tile_nlgp_pa_kernel(tc, x, w_g, out):
         w_scales = keep.tile([P, CHANNELS], U8, name="w_scales", align_bytes=64)
         identity = keep.tile([P, P], F32, name="identity")
 
-        nc.sync.dma_start(out=w_raw[:], in_=w_g.rearrange("(p t) c -> p (t c)", t=PACK))
+        w_rows = w_g.rearrange("(p t) c -> p t c", t=PACK)
+        for first_t in range(0, PACK, 2):
+            nc.sync.dma_start(
+                out=w_raw[:, first_t * CHANNELS : (first_t + 2) * CHANNELS].rearrange("p (t c) -> p t c", t=2),
+                in_=w_rows[:, first_t : first_t + 2, :],
+            )
         for b in images:
             nc.sync.dma_start(out=x_raw[b][:], in_=x[b].rearrange("(q t) h w -> q t (h w)", t=PACK))
         make_identity(nc, identity[:])
@@ -77,13 +83,16 @@ def tile_nlgp_pa_kernel(tc, x, w_g, out):
                 for t in range(2):
                     for u in range(PAIR):
                         nc.tensor.transpose(w_bank[:, t, u, :], w_words[:, first_t + t, u, :], identity[:])
-                target = grouped_words[:, first_t : first_t + 2, :, :]
-                source = w_bank[:].rearrange("q t u p -> q t p u")
-                if first_t == 0:
-                    nc.scalar.copy(out=target, in_=source)
-                else:
-                    nc.vector.tensor_copy(out=target, in_=source)
-            nc.vector.quantize_mx(out=w_codes[:].bitcast(FP8X4), scales=w_scales[:], in_=w_grouped[:])
+                nc.scalar.copy(
+                    out=grouped_words[:, first_t : first_t + 2, :, :],
+                    in_=w_bank[:].rearrange("q t u p -> q t p u"),
+                )
+                d_cols = slice(first_t * P, (first_t + 2) * P)
+                nc.vector.quantize_mx(
+                    out=w_codes[:, d_cols].bitcast(FP8X4),
+                    scales=w_scales[:, d_cols],
+                    in_=w_grouped[:, first_t * P * PACK : (first_t + 2) * P * PACK],
+                )
 
         def project(b):
             for h in range(HALVES):
@@ -129,12 +138,6 @@ def tile_nlgp_pa_kernel(tc, x, w_g, out):
             if b2 == IMAGES - 1:
                 nc.sync.dma_start(out=out.rearrange("(h p) b j -> p h b j", p=P)[:, :, b1, :], in_=best[b1][:])
 
-        def gram_step(s):
-            for k in range(s):
-                gram_block(k, s)
-                gram_block(s, k)
-            gram_block(s, s)
-
         regroup_x(0)
         quantise_w()
         for b in range(X_AHEAD):
@@ -144,12 +147,18 @@ def tile_nlgp_pa_kernel(tc, x, w_g, out):
             project(b)
         quantise_g(0)
         for s in images:
-            if s + X_AHEAD + 1 < IMAGES:
-                regroup_x(s + X_AHEAD + 1)
+            regroup_next = s + X_AHEAD + 1
+            if regroup_next < VECTOR_REGROUPS:
+                regroup_x(regroup_next)
             if s + X_AHEAD < IMAGES:
                 quantise_x(s + X_AHEAD)
-            if s + G_AHEAD < IMAGES:
-                project(s + G_AHEAD)
             if s + 1 < IMAGES:
                 quantise_g(s + 1)
-            gram_step(s)
+            gram_block(s, 0)
+            if s + G_AHEAD < IMAGES:
+                project(s + G_AHEAD)
+            for k in range(s):
+                gram_block(k, s)
+                gram_block(s, k + 1)
+            if VECTOR_REGROUPS <= regroup_next < IMAGES:
+                regroup_x(regroup_next)

@@ -8,6 +8,8 @@ BF16 = mybir.dt.bfloat16
 U32 = mybir.dt.uint32
 U8 = mybir.dt.uint8
 FP8X4 = mybir.dt.float8_e4m3fn_x4
+ALU = mybir.AluOpType
+RELU = mybir.ActivationFunctionType.Relu
 
 P = 128
 PACK = 4
@@ -19,20 +21,22 @@ PAIR = 2
 
 FLOPS = 2 * IMAGES * PIXELS * CHANNELS * (CHANNELS + IMAGES * PIXELS)
 
-STAGE1_BANKS = 3
-STAGE2_BANKS = 5
+SCALAR_BANKS = 4
+VECTOR_BANKS = 4
 RUN = 4
-VECTOR_REGROUPS = 6
-X_AHEAD = 3
-G_AHEAD = 2
+CHAIN = (1, 1, 1, 3, 3, 3, 3, 3)
+NEGATED = (1,)
+SCALAR_RELU = ()
+X_AHEAD = 4
 
 
 def tile_nlgp_pa_kernel(tc, x, w_g, out):
     nc = tc.nc
     with ExitStack() as ctx:
         keep = ctx.enter_context(tc.tile_pool(name="keep", bufs=1))
-        psum_stage1 = ctx.enter_context(tc.psum_pool(name="psum_stage1", bufs=STAGE1_BANKS))
-        psum_stage2 = ctx.enter_context(tc.psum_pool(name="psum_stage2", bufs=STAGE2_BANKS))
+        work = ctx.enter_context(tc.tile_pool(name="work", bufs=4))
+        psum_scalar = ctx.enter_context(tc.psum_pool(name="psum_scalar", bufs=SCALAR_BANKS))
+        psum_vector = ctx.enter_context(tc.psum_pool(name="psum_vector", bufs=VECTOR_BANKS))
         ctx.enter_context(tc.manual_schedule())
 
         images = range(IMAGES)
@@ -43,6 +47,9 @@ def tile_nlgp_pa_kernel(tc, x, w_g, out):
         g_grouped = [keep.tile([P, PIXELS, PACK], BF16, name="g_grouped%d" % b, align_bytes=64) for b in images]
         g_codes = [keep.tile([P, PIXELS], U32, name="g_codes%d" % b, align_bytes=64) for b in images]
         g_scales = [keep.tile([P, PIXELS], U8, name="g_scales%d" % b, align_bytes=64) for b in images]
+        n_grouped = [keep.tile([P, PIXELS, PACK], BF16, name="n_grouped%d" % b, align_bytes=64) for b in NEGATED]
+        n_codes = [keep.tile([P, PIXELS], U32, name="n_codes%d" % b, align_bytes=64) for b in NEGATED]
+        n_scales = [keep.tile([P, PIXELS], U8, name="n_scales%d" % b, align_bytes=64) for b in NEGATED]
         best = [keep.tile([P, HALVES, PIXELS], F32, name="best%d" % b) for b in images]
         w_raw = keep.tile([P, PACK * CHANNELS], BF16, name="w_raw")
         w_grouped = keep.tile([P, CHANNELS * PACK], BF16, name="w_grouped", align_bytes=64)
@@ -50,23 +57,33 @@ def tile_nlgp_pa_kernel(tc, x, w_g, out):
         w_scales = keep.tile([P, CHANNELS], U8, name="w_scales", align_bytes=64)
         identity = keep.tile([P, P], F32, name="identity")
 
-        w_rows = w_g.rearrange("(p t) c -> p t c", t=PACK)
-        for first_t in range(0, PACK, 2):
+        def load_w(half):
+            first_t = 2 * half
             nc.sync.dma_start(
                 out=w_raw[:, first_t * CHANNELS : (first_t + 2) * CHANNELS].rearrange("p (t c) -> p t c", t=2),
-                in_=w_rows[:, first_t : first_t + 2, :],
+                in_=w_g.rearrange("(p t) c -> p t c", t=PACK)[:, first_t : first_t + 2, :],
             )
-        for b in images:
+
+        def load_x(b):
             nc.sync.dma_start(out=x_raw[b][:], in_=x[b].rearrange("(q t) h w -> q t (h w)", t=PACK))
+
+        load_w(0)
+        load_x(0)
+        load_w(1)
+        load_x(1)
+        load_x(2)
+        load_x(3)
+        load_x(4)
+        load_x(5)
+        load_x(6)
+        load_x(7)
         make_identity(nc, identity[:])
 
         def regroup_x(b):
-            source = x_raw[b][:].rearrange("q t (n i) -> q n t i", i=RUN)
-            target = x_grouped[b][:].rearrange("q (n i) t -> q n t i", i=RUN)
-            if b < VECTOR_REGROUPS:
-                nc.vector.tensor_copy(out=target, in_=source)
-            else:
-                nc.scalar.copy(out=target, in_=source)
+            nc.vector.tensor_copy(
+                out=x_grouped[b][:].rearrange("q (n i) t -> q n t i", i=RUN),
+                in_=x_raw[b][:].rearrange("q t (n i) -> q n t i", i=RUN),
+            )
 
         def quantise_x(b):
             nc.vector.quantize_mx(
@@ -75,40 +92,45 @@ def tile_nlgp_pa_kernel(tc, x, w_g, out):
                 in_=x_grouped[b][:].rearrange("q i t -> q (i t)"),
             )
 
-        def quantise_w():
+        def transpose_w(half):
             w_words = w_raw[:].bitcast(F32).rearrange("p (t q u) -> p t u q", t=PACK, u=PAIR)
             grouped_words = w_grouped[:].bitcast(F32).rearrange("q (t p u) -> q t p u", t=PACK, u=PAIR)
-            for first_t in range(0, PACK, 2):
-                w_bank = psum_stage1.tile([P, 2, PAIR, P], F32, tag="bank")
-                for t in range(2):
-                    for u in range(PAIR):
-                        nc.tensor.transpose(w_bank[:, t, u, :], w_words[:, first_t + t, u, :], identity[:])
-                nc.scalar.copy(
-                    out=grouped_words[:, first_t : first_t + 2, :, :],
-                    in_=w_bank[:].rearrange("q t u p -> q t p u"),
-                )
-                d_cols = slice(first_t * P, (first_t + 2) * P)
-                nc.vector.quantize_mx(
-                    out=w_codes[:, d_cols].bitcast(FP8X4),
-                    scales=w_scales[:, d_cols],
-                    in_=w_grouped[:, first_t * P * PACK : (first_t + 2) * P * PACK],
-                )
+            w_bank = psum_scalar.tile([P, 2, PAIR, P], F32, name="w_bank", tag="bank")
+            for t in range(2):
+                for u in range(PAIR):
+                    nc.tensor.transpose(w_bank[:, t, u, :], w_words[:, 2 * half + t, u, :], identity[:])
+            target = grouped_words[:, 2 * half : 2 * half + 2, :, :]
+            source = w_bank[:].rearrange("q t u p -> q t p u")
+            if half in ():
+                nc.vector.tensor_copy(out=target, in_=source)
+            else:
+                nc.scalar.copy(out=target, in_=source)
 
-        def project(b):
-            for h in range(HALVES):
-                pixels = slice(h * P, (h + 1) * P)
-                g_bank = psum_stage1.tile([P, PACK, P], F32, tag="bank")
-                for t in range(PACK):
-                    d_cols = slice(t * P, (t + 1) * P)
-                    nc.tensor.matmul_mx(
-                        out=g_bank[:, t, :],
-                        lhsT=w_codes[:, d_cols].bitcast(FP8X4),
-                        lhsT_scale=w_scales[:, d_cols],
-                        rhs=x_codes[b][:, pixels].bitcast(FP8X4),
-                        rhs_scale=x_scales[b][:, pixels],
-                        start=True,
-                        stop=True,
-                    )
+        def quantise_w(half):
+            d_cols = slice(2 * half * P, (2 * half + 2) * P)
+            nc.vector.quantize_mx(
+                out=w_codes[:, d_cols].bitcast(FP8X4),
+                scales=w_scales[:, d_cols],
+                in_=w_grouped[:, 2 * half * P * PACK : (2 * half + 2) * P * PACK],
+            )
+
+        def project(b, h):
+            pixels = slice(h * P, (h + 1) * P)
+            g_bank = psum_scalar.tile([P, PACK, P], F32, name="g_bank", tag="bank")
+            for t in range(PACK):
+                d_cols = slice(t * P, (t + 1) * P)
+                nc.tensor.matmul_mx(
+                    out=g_bank[:, t, :],
+                    lhsT=w_codes[:, d_cols].bitcast(FP8X4),
+                    lhsT_scale=w_scales[:, d_cols],
+                    rhs=x_codes[b][:, pixels].bitcast(FP8X4),
+                    rhs_scale=x_scales[b][:, pixels],
+                    start=True,
+                    stop=True,
+                )
+            if (b, h) in ():
+                nc.vector.tensor_copy(out=g_grouped[b][:, pixels, :], in_=g_bank[:].rearrange("p t i -> p i t"))
+            else:
                 nc.scalar.copy(out=g_grouped[b][:, pixels, :], in_=g_bank[:].rearrange("p t i -> p i t"))
 
         def quantise_g(b):
@@ -118,47 +140,172 @@ def tile_nlgp_pa_kernel(tc, x, w_g, out):
                 in_=g_grouped[b][:].rearrange("p i t -> p (i t)"),
             )
 
-        def gram_block(b1, b2):
-            p_bank = psum_stage2.tile([P, HALVES, PIXELS], F32, tag="bank")
+        def negate_g(b):
+            n = NEGATED.index(b)
+            nc.vector.tensor_scalar(out=n_grouped[n][:], in0=g_grouped[b][:], scalar1=-1.0, scalar2=None, op0=ALU.mult)
+
+        def quantise_negated(b):
+            n = NEGATED.index(b)
+            nc.vector.quantize_mx(
+                out=n_codes[n][:].bitcast(FP8X4),
+                scales=n_scales[n][:],
+                in_=n_grouped[n][:].rearrange("p i t -> p (i t)"),
+            )
+
+        def gram(bank, b1, plus, minus=None):
+            moving = [(g_codes[plus], g_scales[plus])]
+            if minus is not None:
+                moving.append((n_codes[NEGATED.index(minus)], n_scales[NEGATED.index(minus)]))
             for h in range(HALVES):
                 rows = slice(h * P, (h + 1) * P)
-                nc.tensor.matmul_mx(
-                    out=p_bank[:, h, :],
-                    lhsT=g_codes[b1][:, rows].bitcast(FP8X4),
-                    lhsT_scale=g_scales[b1][:, rows],
-                    rhs=g_codes[b2][:].bitcast(FP8X4),
-                    rhs_scale=g_scales[b2][:],
-                    start=True,
-                    stop=True,
-                )
-            if b2 == 0:
-                nc.scalar.copy(out=best[b1][:], in_=p_bank[:])
-            else:
-                nc.vector.tensor_tensor(out=best[b1][:], in0=p_bank[:], in1=best[b1][:], op=mybir.AluOpType.max)
-            if b2 == IMAGES - 1:
-                nc.sync.dma_start(out=out.rearrange("(h p) b j -> p h b j", p=P)[:, :, b1, :], in_=best[b1][:])
+                for n, (codes, scales) in enumerate(moving):
+                    nc.tensor.matmul_mx(
+                        out=bank[:, h, :],
+                        lhsT=g_codes[b1][:, rows].bitcast(FP8X4),
+                        lhsT_scale=g_scales[b1][:, rows],
+                        rhs=codes[:].bitcast(FP8X4),
+                        rhs_scale=scales[:],
+                        start=(n == 0),
+                        stop=(n == len(moving) - 1),
+                    )
 
+        def scalar_bank():
+            p_bank = psum_scalar.tile([P, HALVES, PIXELS], F32, name="s_bank", tag="bank")
+            return p_bank
+
+        excess = {}
+
+        def row_first(b1):
+            p_bank = scalar_bank()
+            if CHAIN[b1] == 1:
+                gram(p_bank, b1, 0)
+                nc.scalar.copy(out=best[b1][:], in_=p_bank[:])
+                return
+            gram(p_bank, b1, 0, 1)
+            e = work.tile([P, HALVES, PIXELS], F32, name="e", tag="excess")
+            nc.scalar.activation(out=e[:], in_=p_bank[:], func=RELU)
+            excess[b1] = e
+
+        def row_middle(b1, n):
+            p_bank = scalar_bank()
+            if n - 1 in NEGATED:
+                gram(p_bank, b1, n, n - 1)
+            else:
+                gram(p_bank, b1, n - 1, n)
+            d = work.tile([P, HALVES, PIXELS], F32, name="d", tag="difference")
+            nc.scalar.copy(out=d[:], in_=p_bank[:])
+            s = work.tile([P, HALVES, PIXELS], F32, name="s", tag="shifted")
+            nc.gpsimd.tensor_tensor(out=s[:], in0=excess[b1][:], in1=d[:], op=ALU.subtract if n - 1 in NEGATED else ALU.add)
+            e = work.tile([P, HALVES, PIXELS], F32, name="e", tag="excess")
+            excess[b1] = e
+            if b1 in SCALAR_RELU:
+                return (s, e)
+            nc.gpsimd.tensor_scalar(out=e[:], in0=s[:], scalar1=0.0, scalar2=0.0, op0=ALU.max, op1=ALU.add)
+
+        def row_relu(b1, pair):
+            nc.scalar.activation(out=pair[1][:], in_=pair[0][:], func=RELU)
+
+        def row_last(b1):
+            p_bank = scalar_bank()
+            gram(p_bank, b1, CHAIN[b1] - 1)
+            base = work.tile([P, HALVES, PIXELS], F32, name="base", tag="base")
+            nc.scalar.copy(out=base[:], in_=p_bank[:])
+            return base
+
+        def row_add(b1, base):
+            nc.gpsimd.tensor_tensor(out=best[b1][:], in0=excess[b1][:], in1=base[:], op=ALU.add)
+
+        scalar_items = []
+
+        def add_project(b):
+            for h in range(HALVES):
+                scalar_items.append(("project", b, lambda h=h: project(b, h)))
+
+        def start_row(b):
+            if CHAIN[b] == 1:
+                scalar_items.append(("row", b, lambda: row_first(b)))
+                return
+            held = {}
+            scalar_items.append(("part", b, lambda: row_first(b)))
+            for n in range(2, CHAIN[b]):
+                def middle(n=n):
+                    held[n] = row_middle(b, n)
+                scalar_items.append(("part", b, middle))
+                if b in SCALAR_RELU:
+                    def relu(n=n):
+                        row_relu(b, held[n])
+                    if n == CHAIN[b] - 1:
+                        def last_base():
+                            held[0] = row_last(b)
+                        scalar_items.append(("part", b, last_base))
+                        def last_relu(n=n):
+                            row_relu(b, held[n])
+                            row_add(b, held[0])
+                        scalar_items.append(("row", b, last_relu))
+                    else:
+                        scalar_items.append(("part", b, relu))
+            if b not in SCALAR_RELU or CHAIN[b] == 2:
+                scalar_items.append(("row", b, lambda: row_add(b, row_last(b))))
+
+        for item, b in [(add_project, 0), (add_project, 1), (start_row, 0), (add_project, 2), (start_row, 1), (add_project, 3), (start_row, 2), (add_project, 4), (add_project, 5), (start_row, 3), (add_project, 6), (start_row, 4), (add_project, 7), (start_row, 5), (start_row, 6), (start_row, 7)]:
+            item(b)
+
+        def feed(count):
+            for n in range(min(count, len(scalar_items))):
+                kind, b, item = scalar_items.pop(0)
+                item()
+
+        def feed_until(kind, b):
+            while [i for i in scalar_items if i[0] == kind and i[1] == b]:
+                feed(1)
+
+        done = [0] * IMAGES
+
+        def maximum(b1, b2):
+            feed_until("row", b1)
+            p_bank = psum_vector.tile([P, HALVES, PIXELS], F32, name="p_bank", tag="bank")
+            gram(p_bank, b1, b2)
+            nc.vector.tensor_tensor(out=best[b1][:], in0=p_bank[:], in1=best[b1][:], op=ALU.max)
+            done[b1] += 1
+            if done[b1] == IMAGES - CHAIN[b1]:
+                nc.sync.dma_start(out=out.rearrange("(h p) b j -> p h b j", p=P)[:, :, b1, :], in_=best[b1][:])
+            feed(1)
+
+        transpose_w(0)
         regroup_x(0)
-        quantise_w()
-        for b in range(X_AHEAD):
+        transpose_w(1)
+        quantise_w(0)
+        quantise_x(0)
+        regroup_x(1)
+        quantise_w(1)
+        for b in range(1, X_AHEAD):
             regroup_x(b + 1)
             quantise_x(b)
-        for b in range(G_AHEAD):
-            project(b)
+        feed_until("project", 0)
         quantise_g(0)
+        feed(1)
+        direct = [b for b in images if CHAIN[b] == 1]
         for s in images:
-            regroup_next = s + X_AHEAD + 1
-            if regroup_next < VECTOR_REGROUPS:
-                regroup_x(regroup_next)
+            if s + 1 < IMAGES:
+                feed_until("project", s + 1)
+                quantise_g(s + 1)
+                feed(1)
+                if s + 1 in NEGATED:
+                    negate_g(s + 1)
+            if s + X_AHEAD + 1 < IMAGES:
+                regroup_x(s + X_AHEAD + 1)
+            if s + 1 in NEGATED:
+                quantise_negated(s + 1)
             if s + X_AHEAD < IMAGES:
                 quantise_x(s + X_AHEAD)
-            if s + 1 < IMAGES:
-                quantise_g(s + 1)
-            gram_block(s, 0)
-            if s + G_AHEAD < IMAGES:
-                project(s + G_AHEAD)
-            for k in range(s):
-                gram_block(k, s)
-                gram_block(s, k + 1)
-            if VECTOR_REGROUPS <= regroup_next < IMAGES:
-                regroup_x(regroup_next)
+                feed(0)
+            for r in direct:
+                if r < s:
+                    maximum(r, s)
+                    if s in direct:
+                        maximum(s, r + 1)
+        for group in ((3, 4), (5, 6, 7)):
+            for b2 in images:
+                for r in group:
+                    if b2 >= CHAIN[r]:
+                        maximum(r, b2)

@@ -24,9 +24,9 @@ FLOPS = 2 * IMAGES * PIXELS * CHANNELS * (CHANNELS + IMAGES * PIXELS)
 SCALAR_BANKS = 4
 VECTOR_BANKS = 4
 RUN = 4
-CHAIN = (1, 1, 1, 3, 3, 3, 3, 3)
+CHAIN = (1, 1, 1, 2, 2, 3, 3, 3)
 NEGATED = (1,)
-SCALAR_RELU = ()
+SCALAR_RELU = (3, 4, 5, 6, 7)
 X_AHEAD = 4
 
 

@@ -24,9 +24,9 @@ FLOPS = 2 * IMAGES * PIXELS * CHANNELS * (CHANNELS + IMAGES * PIXELS)
 SCALAR_BANKS = 4
 VECTOR_BANKS = 4
 RUN = 4
-CHAIN = (1, 1, 1, 2, 2, 3, 3, 3)
-NEGATED = (1,)
-SCALAR_RELU = (3, 4, 5, 6, 7)
+CHAIN = (1, 1, 1, 3, 3, 3, 4, 5)
+NEGATED = (1, 3)
+SCALAR_RELU = (0,1,2,3,4,5,6,7)
 X_AHEAD = 4
 
 
@@ -68,8 +68,8 @@ def tile_nlgp_pa_kernel(tc, x, w_g, out):
             nc.sync.dma_start(out=x_raw[b][:], in_=x[b].rearrange("(q t) h w -> q t (h w)", t=PACK))
 
         load_w(0)
-        load_x(0)
         load_w(1)
+        load_x(0)
         load_x(1)
         load_x(2)
         load_x(3)
@@ -217,38 +217,40 @@ def tile_nlgp_pa_kernel(tc, x, w_g, out):
 
         scalar_items = []
 
-        def add_project(b):
-            for h in range(HALVES):
-                scalar_items.append(("project", b, lambda h=h: project(b, h)))
-
-        def start_row(b):
-            if CHAIN[b] == 1:
-                scalar_items.append(("row", b, lambda: row_first(b)))
-                return
+        def segments(b):
+            length = CHAIN[b]
+            if length == 1:
+                return [[lambda: row_first(b)]]
             held = {}
-            scalar_items.append(("part", b, lambda: row_first(b)))
-            for n in range(2, CHAIN[b]):
+            result = [[lambda: row_first(b)]]
+            for n in range(2, length):
                 def middle(n=n):
                     held[n] = row_middle(b, n)
-                scalar_items.append(("part", b, middle))
-                if b in SCALAR_RELU:
-                    def relu(n=n):
-                        row_relu(b, held[n])
-                    if n == CHAIN[b] - 1:
-                        def last_base():
-                            held[0] = row_last(b)
-                        scalar_items.append(("part", b, last_base))
-                        def last_relu(n=n):
-                            row_relu(b, held[n])
-                            row_add(b, held[0])
-                        scalar_items.append(("row", b, last_relu))
-                    else:
-                        scalar_items.append(("part", b, relu))
-            if b not in SCALAR_RELU or CHAIN[b] == 2:
-                scalar_items.append(("row", b, lambda: row_add(b, row_last(b))))
+                def relu(n=n):
+                    row_relu(b, held[n])
+                result[-1].append(middle)
+                result.append([relu])
+            def copy():
+                held[0] = row_last(b)
+            def finish():
+                if length > 2:
+                    row_relu(b, held[length - 1])
+                row_add(b, held[0])
+            result[-1] = result[-1][:-1] if length > 2 else result[-1]
+            result[-1].append(copy)
+            result[-1].append(finish)
+            return result
 
-        for item, b in [(add_project, 0), (add_project, 1), (start_row, 0), (add_project, 2), (start_row, 1), (add_project, 3), (start_row, 2), (add_project, 4), (add_project, 5), (start_row, 3), (add_project, 6), (start_row, 4), (add_project, 7), (start_row, 5), (start_row, 6), (start_row, 7)]:
-            item(b)
+        rows = {b: segments(b) for b in images}
+        for word in "p0 p1 r0 p2 r1 p3 r2 p4 p5 r3 p6 r3 r4 p7 r4 r5 r6 r5 r7 r6 r7 r6 r7 r7".split(" "):
+            b = int(word[1:])
+            if word[0] == "p":
+                for h in range(HALVES):
+                    scalar_items.append(("project", b, lambda b=b, h=h: project(b, h)))
+            else:
+                for item in rows[b].pop(0):
+                    scalar_items.append(("row", b, item))
+        assert all([not r for r in rows.values()])
 
         def feed(count):
             for n in range(min(count, len(scalar_items))):
@@ -260,35 +262,69 @@ def tile_nlgp_pa_kernel(tc, x, w_g, out):
                 feed(1)
 
         done = [0] * IMAGES
+        direct = [b for b in images if CHAIN[b] == 1]
+        maxima = []
+        for s in images:
+            for r in direct:
+                if r < s:
+                    maxima.append((r, s))
+                    if s in direct:
+                        maxima.append((s, r + 1))
+        for group in ((3, 4, 5), (6, 7)):
+            for b2 in images:
+                for r in group:
+                    if b2 >= CHAIN[r]:
+                        maxima.append((r, b2))
+        quantised = set()
+        banks = []
+        count = [0]
+
+        def grams(limit):
+            while len(banks) < min(limit, len(maxima)) and all([b in quantised for b in maxima[len(banks)]]):
+                b1, b2 = maxima[len(banks)]
+                p_bank = psum_vector.tile([P, HALVES, PIXELS], F32, name="p_bank", tag="bank")
+                gram(p_bank, b1, b2)
+                banks.append(p_bank)
 
         def maximum(b1, b2):
             feed_until("row", b1)
-            p_bank = psum_vector.tile([P, HALVES, PIXELS], F32, name="p_bank", tag="bank")
-            gram(p_bank, b1, b2)
-            nc.vector.tensor_tensor(out=best[b1][:], in0=p_bank[:], in1=best[b1][:], op=ALU.max)
+            n = count[0]
+            assert maxima[n] == (b1, b2)
+            grams(n + 1 + 0)
             done[b1] += 1
-            if done[b1] == IMAGES - CHAIN[b1]:
-                nc.sync.dma_start(out=out.rearrange("(h p) b j -> p h b j", p=P)[:, :, b1, :], in_=best[b1][:])
+            whole = out.rearrange("(h p) b j -> p h b j", p=P)[:, :, b1, :]
+            if n == len(maxima) - 1:
+                for h in range(HALVES):
+                    nc.vector.tensor_tensor(out=best[b1][:, h, :], in0=banks[n][:, h, :], in1=best[b1][:, h, :], op=ALU.max)
+                    nc.sync.dma_start(out=whole[:, h, :], in_=best[b1][:, h, :])
+            else:
+                nc.vector.tensor_tensor(out=best[b1][:], in0=banks[n][:], in1=best[b1][:], op=ALU.max)
+                if done[b1] == IMAGES - CHAIN[b1]:
+                    nc.sync.dma_start(out=whole, in_=best[b1][:])
+            count[0] += 1
             feed(1)
 
         transpose_w(0)
-        regroup_x(0)
         transpose_w(1)
+        regroup_x(0)
         quantise_w(0)
         quantise_x(0)
-        regroup_x(1)
         quantise_w(1)
+        regroup_x(1)
         for b in range(1, X_AHEAD):
             regroup_x(b + 1)
             quantise_x(b)
         feed_until("project", 0)
         quantise_g(0)
+        quantised.add(0)
         feed(1)
         direct = [b for b in images if CHAIN[b] == 1]
         for s in images:
             if s + 1 < IMAGES:
                 feed_until("project", s + 1)
                 quantise_g(s + 1)
+                quantised.add(s + 1)
+                grams(count[0] + 0)
                 feed(1)
                 if s + 1 in NEGATED:
                     negate_g(s + 1)
@@ -304,7 +340,7 @@ def tile_nlgp_pa_kernel(tc, x, w_g, out):
                     maximum(r, s)
                     if s in direct:
                         maximum(s, r + 1)
-        for group in ((3, 4), (5, 6, 7)):
+        for group in ((3, 4, 5), (6, 7)):
             for b2 in images:
                 for r in group:
                     if b2 >= CHAIN[r]:

@@ -9,6 +9,7 @@ U32 = mybir.dt.uint32
 U8 = mybir.dt.uint8
 FP8X4 = mybir.dt.float8_e4m3fn_x4
 ALU = mybir.AluOpType
+COPY = mybir.ActivationFunctionType.Copy
 RELU = mybir.ActivationFunctionType.Relu
 
 P = 128
@@ -24,10 +25,9 @@ FLOPS = 2 * IMAGES * PIXELS * CHANNELS * (CHANNELS + IMAGES * PIXELS)
 SCALAR_BANKS = 4
 VECTOR_BANKS = 4
 RUN = 4
-CHAIN = (1, 1, 1, 3, 3, 3, 4, 5)
-NEGATED = (1, 3)
-SCALAR_RELU = (0,1,2,3,4,5,6,7)
-X_AHEAD = 4
+START = (1, 1, 1, 3, 2, 2, 4, 5)
+X_AHEAD = 5
+SIGN = (1, -1) * (IMAGES // 2)
 
 
 def tile_nlgp_pa_kernel(tc, x, w_g, out):
@@ -47,9 +47,6 @@ def tile_nlgp_pa_kernel(tc, x, w_g, out):
         g_grouped = [keep.tile([P, PIXELS, PACK], BF16, name="g_grouped%d" % b, align_bytes=64) for b in images]
         g_codes = [keep.tile([P, PIXELS], U32, name="g_codes%d" % b, align_bytes=64) for b in images]
         g_scales = [keep.tile([P, PIXELS], U8, name="g_scales%d" % b, align_bytes=64) for b in images]
-        n_grouped = [keep.tile([P, PIXELS, PACK], BF16, name="n_grouped%d" % b, align_bytes=64) for b in NEGATED]
-        n_codes = [keep.tile([P, PIXELS], U32, name="n_codes%d" % b, align_bytes=64) for b in NEGATED]
-        n_scales = [keep.tile([P, PIXELS], U8, name="n_scales%d" % b, align_bytes=64) for b in NEGATED]
         best = [keep.tile([P, HALVES, PIXELS], F32, name="best%d" % b) for b in images]
         w_raw = keep.tile([P, PACK * CHANNELS], BF16, name="w_raw")
         w_grouped = keep.tile([P, CHANNELS * PACK], BF16, name="w_grouped", align_bytes=64)
@@ -80,10 +77,12 @@ def tile_nlgp_pa_kernel(tc, x, w_g, out):
         make_identity(nc, identity[:])
 
         def regroup_x(b):
-            nc.vector.tensor_copy(
-                out=x_grouped[b][:].rearrange("q (n i) t -> q n t i", i=RUN),
-                in_=x_raw[b][:].rearrange("q t (n i) -> q n t i", i=RUN),
-            )
+            target = x_grouped[b][:].rearrange("q (n i) t -> q n t i", i=RUN)
+            source = x_raw[b][:].rearrange("q t (n i) -> q n t i", i=RUN)
+            if b in ():
+                nc.gpsimd.tensor_scalar(out=target, in0=source, scalar1=1.0, scalar2=0.0, op0=ALU.mult, op1=ALU.add)
+            else:
+                nc.vector.tensor_copy(out=target, in_=source)
 
         def quantise_x(b):
             nc.vector.quantize_mx(
@@ -99,12 +98,9 @@ def tile_nlgp_pa_kernel(tc, x, w_g, out):
             for t in range(2):
                 for u in range(PAIR):
                     nc.tensor.transpose(w_bank[:, t, u, :], w_words[:, 2 * half + t, u, :], identity[:])
-            target = grouped_words[:, 2 * half : 2 * half + 2, :, :]
-            source = w_bank[:].rearrange("q t u p -> q t p u")
-            if half in ():
-                nc.vector.tensor_copy(out=target, in_=source)
-            else:
-                nc.scalar.copy(out=target, in_=source)
+            nc.scalar.copy(
+                out=grouped_words[:, 2 * half : 2 * half + 2, :, :], in_=w_bank[:].rearrange("q t u p -> q t p u")
+            )
 
         def quantise_w(half):
             d_cols = slice(2 * half * P, (2 * half + 2) * P)
@@ -128,10 +124,14 @@ def tile_nlgp_pa_kernel(tc, x, w_g, out):
                     start=True,
                     stop=True,
                 )
+            source = g_bank[:].rearrange("p t i -> p i t")
             if (b, h) in ():
-                nc.vector.tensor_copy(out=g_grouped[b][:, pixels, :], in_=g_bank[:].rearrange("p t i -> p i t"))
+                assert SIGN[b] > 0
+                nc.vector.tensor_copy(out=g_grouped[b][:, pixels, :], in_=source)
+            elif SIGN[b] > 0:
+                nc.scalar.copy(out=g_grouped[b][:, pixels, :], in_=source)
             else:
-                nc.scalar.copy(out=g_grouped[b][:, pixels, :], in_=g_bank[:].rearrange("p t i -> p i t"))
+                nc.scalar.activation(out=g_grouped[b][:, pixels, :], in_=source, func=COPY, scale=-1.0)
 
         def quantise_g(b):
             nc.vector.quantize_mx(
@@ -140,168 +140,135 @@ def tile_nlgp_pa_kernel(tc, x, w_g, out):
                 in_=g_grouped[b][:].rearrange("p i t -> p (i t)"),
             )
 
-        def negate_g(b):
-            n = NEGATED.index(b)
-            nc.vector.tensor_scalar(out=n_grouped[n][:], in0=g_grouped[b][:], scalar1=-1.0, scalar2=None, op0=ALU.mult)
-
-        def quantise_negated(b):
-            n = NEGATED.index(b)
-            nc.vector.quantize_mx(
-                out=n_codes[n][:].bitcast(FP8X4),
-                scales=n_scales[n][:],
-                in_=n_grouped[n][:].rearrange("p i t -> p (i t)"),
-            )
-
-        def gram(bank, b1, plus, minus=None):
-            moving = [(g_codes[plus], g_scales[plus])]
-            if minus is not None:
-                moving.append((n_codes[NEGATED.index(minus)], n_scales[NEGATED.index(minus)]))
+        def gram(bank, b1, partners):
             for h in range(HALVES):
                 rows = slice(h * P, (h + 1) * P)
-                for n, (codes, scales) in enumerate(moving):
+                for n, b2 in enumerate(partners):
                     nc.tensor.matmul_mx(
                         out=bank[:, h, :],
                         lhsT=g_codes[b1][:, rows].bitcast(FP8X4),
                         lhsT_scale=g_scales[b1][:, rows],
-                        rhs=codes[:].bitcast(FP8X4),
-                        rhs_scale=scales[:],
+                        rhs=g_codes[b2][:].bitcast(FP8X4),
+                        rhs_scale=g_scales[b2][:],
                         start=(n == 0),
-                        stop=(n == len(moving) - 1),
+                        stop=(n == len(partners) - 1),
                     )
 
-        def scalar_bank():
+        def scalar_gram(b1, partners):
             p_bank = psum_scalar.tile([P, HALVES, PIXELS], F32, name="s_bank", tag="bank")
+            gram(p_bank, b1, partners)
             return p_bank
 
         excess = {}
+        shifted = {}
+        base = {}
 
         def row_first(b1):
-            p_bank = scalar_bank()
-            if CHAIN[b1] == 1:
-                gram(p_bank, b1, 0)
-                nc.scalar.copy(out=best[b1][:], in_=p_bank[:])
+            if START[b1] == 1:
+                p_bank = scalar_gram(b1, [0])
+                if SIGN[b1] > 0:
+                    nc.scalar.copy(out=best[b1][:], in_=p_bank[:])
+                else:
+                    nc.scalar.activation(out=best[b1][:], in_=p_bank[:], func=COPY, scale=-1.0)
                 return
-            gram(p_bank, b1, 0, 1)
+            p_bank = scalar_gram(b1, [0, 1])
             e = work.tile([P, HALVES, PIXELS], F32, name="e", tag="excess")
-            nc.scalar.activation(out=e[:], in_=p_bank[:], func=RELU)
+            nc.scalar.activation(out=e[:], in_=p_bank[:], func=RELU, scale=float(SIGN[b1]))
             excess[b1] = e
 
-        def row_middle(b1, n):
-            p_bank = scalar_bank()
-            if n - 1 in NEGATED:
-                gram(p_bank, b1, n, n - 1)
-            else:
-                gram(p_bank, b1, n - 1, n)
+        def row_step(b1, n):
+            p_bank = scalar_gram(b1, [n - 1, n])
             d = work.tile([P, HALVES, PIXELS], F32, name="d", tag="difference")
             nc.scalar.copy(out=d[:], in_=p_bank[:])
             s = work.tile([P, HALVES, PIXELS], F32, name="s", tag="shifted")
-            nc.gpsimd.tensor_tensor(out=s[:], in0=excess[b1][:], in1=d[:], op=ALU.subtract if n - 1 in NEGATED else ALU.add)
+            op = ALU.add if SIGN[b1] * SIGN[n - 1] > 0 else ALU.subtract
+            nc.gpsimd.tensor_tensor(out=s[:], in0=excess[b1][:], in1=d[:], op=op)
+            shifted[b1] = s
+
+        def row_relu(b1):
             e = work.tile([P, HALVES, PIXELS], F32, name="e", tag="excess")
+            nc.scalar.activation(out=e[:], in_=shifted[b1][:], func=RELU)
             excess[b1] = e
-            if b1 in SCALAR_RELU:
-                return (s, e)
-            nc.gpsimd.tensor_scalar(out=e[:], in0=s[:], scalar1=0.0, scalar2=0.0, op0=ALU.max, op1=ALU.add)
 
-        def row_relu(b1, pair):
-            nc.scalar.activation(out=pair[1][:], in_=pair[0][:], func=RELU)
+        def row_base(b1):
+            p_bank = scalar_gram(b1, [START[b1] - 1])
+            c = work.tile([P, HALVES, PIXELS], F32, name="c", tag="base")
+            nc.scalar.copy(out=c[:], in_=p_bank[:])
+            base[b1] = c
 
-        def row_last(b1):
-            p_bank = scalar_bank()
-            gram(p_bank, b1, CHAIN[b1] - 1)
-            base = work.tile([P, HALVES, PIXELS], F32, name="base", tag="base")
-            nc.scalar.copy(out=base[:], in_=p_bank[:])
-            return base
-
-        def row_add(b1, base):
-            nc.gpsimd.tensor_tensor(out=best[b1][:], in0=excess[b1][:], in1=base[:], op=ALU.add)
+        def row_finish(b1):
+            op = ALU.add if SIGN[b1] * SIGN[START[b1] - 1] > 0 else ALU.subtract
+            nc.gpsimd.tensor_tensor(out=best[b1][:], in0=excess[b1][:], in1=base[b1][:], op=op)
 
         scalar_items = []
 
         def segments(b):
-            length = CHAIN[b]
+            length = START[b]
             if length == 1:
-                return [[lambda: row_first(b)]]
-            held = {}
-            result = [[lambda: row_first(b)]]
+                return [[(row_first, b)]]
+            result = [[(row_first, b)]]
             for n in range(2, length):
-                def middle(n=n):
-                    held[n] = row_middle(b, n)
-                def relu(n=n):
-                    row_relu(b, held[n])
-                result[-1].append(middle)
-                result.append([relu])
-            def copy():
-                held[0] = row_last(b)
-            def finish():
-                if length > 2:
-                    row_relu(b, held[length - 1])
-                row_add(b, held[0])
-            result[-1] = result[-1][:-1] if length > 2 else result[-1]
-            result[-1].append(copy)
-            result[-1].append(finish)
+                result[-1].append((row_step, b, n))
+                result.append([(row_relu, b)])
+            if length == 2:
+                result[-1] += [(row_base, b), (row_finish, b)]
+            else:
+                result[-2].append((row_base, b)) if 0 else result[-1].insert(0, (row_base, b))
+                result[-1].append((row_finish, b))
             return result
 
         rows = {b: segments(b) for b in images}
-        for word in "p0 p1 r0 p2 r1 p3 r2 p4 p5 r3 p6 r3 r4 p7 r4 r5 r6 r5 r7 r6 r7 r6 r7 r7".split(" "):
+        for word in "p0 p1 p2 r0 r1 p3 r2 p5 p4 r3 p7 p6 r3 r4 r5 r6 r7 r6 r7 r7 r6 r7".split(" "):
             b = int(word[1:])
             if word[0] == "p":
-                for h in range(HALVES):
-                    scalar_items.append(("project", b, lambda b=b, h=h: project(b, h)))
+                scalar_items += [(project, b, h) for h in range(HALVES)]
             else:
-                for item in rows[b].pop(0):
-                    scalar_items.append(("row", b, item))
+                scalar_items += rows[b].pop(0)
         assert all([not r for r in rows.values()])
 
+        credit = [0.0]
+
+        def issue():
+            item = scalar_items.pop(0)
+            item[0](*item[1:])
+            if item[0] == row_finish:
+                return 0
+            if item[0] == row_relu:
+                return 1
+            return 1.5 if item[0] in (row_step,) or (item[0] == row_first and START[item[1]] > 1) else 1
+
         def feed(count):
-            for n in range(min(count, len(scalar_items))):
-                kind, b, item = scalar_items.pop(0)
-                item()
+            credit[0] = min(credit[0] + count, 2)
+            while credit[0] > 0 and scalar_items:
+                credit[0] -= issue()
 
-        def feed_until(kind, b):
-            while [i for i in scalar_items if i[0] == kind and i[1] == b]:
-                feed(1)
+        def feed_until(kinds, b):
+            while any([i[0] in kinds and i[1] == b for i in scalar_items]):
+                issue()
 
+        direct = [b for b in images if START[b] == 1]
         done = [0] * IMAGES
-        direct = [b for b in images if CHAIN[b] == 1]
-        maxima = []
-        for s in images:
-            for r in direct:
-                if r < s:
-                    maxima.append((r, s))
-                    if s in direct:
-                        maxima.append((s, r + 1))
-        for group in ((3, 4, 5), (6, 7)):
-            for b2 in images:
-                for r in group:
-                    if b2 >= CHAIN[r]:
-                        maxima.append((r, b2))
-        quantised = set()
-        banks = []
-        count = [0]
-
-        def grams(limit):
-            while len(banks) < min(limit, len(maxima)) and all([b in quantised for b in maxima[len(banks)]]):
-                b1, b2 = maxima[len(banks)]
-                p_bank = psum_vector.tile([P, HALVES, PIXELS], F32, name="p_bank", tag="bank")
-                gram(p_bank, b1, b2)
-                banks.append(p_bank)
+        total = [0]
 
         def maximum(b1, b2):
-            feed_until("row", b1)
-            n = count[0]
-            assert maxima[n] == (b1, b2)
-            grams(n + 1 + 0)
+            feed_until((row_first, row_finish), b1)
+            p_bank = psum_vector.tile([P, HALVES, PIXELS], F32, name="p_bank", tag="bank")
+            gram(p_bank, b1, [b2])
+            total[0] += 1
             done[b1] += 1
             whole = out.rearrange("(h p) b j -> p h b j", p=P)[:, :, b1, :]
-            if n == len(maxima) - 1:
-                for h in range(HALVES):
-                    nc.vector.tensor_tensor(out=best[b1][:, h, :], in0=banks[n][:, h, :], in1=best[b1][:, h, :], op=ALU.max)
-                    nc.sync.dma_start(out=whole[:, h, :], in_=best[b1][:, h, :])
-            else:
-                nc.vector.tensor_tensor(out=best[b1][:], in0=banks[n][:], in1=best[b1][:], op=ALU.max)
-                if done[b1] == IMAGES - CHAIN[b1]:
-                    nc.sync.dma_start(out=whole, in_=best[b1][:])
-            count[0] += 1
+            parts = [slice(0, HALVES)]
+            if total[0] == sum([IMAGES - n for n in START]):
+                parts = [slice(h, h + 1) for h in range(HALVES)]
+            for part in parts:
+                if SIGN[b1] * SIGN[b2] > 0:
+                    nc.vector.tensor_tensor(out=best[b1][:, part, :], in0=p_bank[:, part, :], in1=best[b1][:, part, :], op=ALU.max)
+                else:
+                    nc.vector.scalar_tensor_tensor(
+                        out=best[b1][:, part, :], in0=p_bank[:, part, :], scalar=-1.0, in1=best[b1][:, part, :], op0=ALU.mult, op1=ALU.max
+                    )
+                if done[b1] == IMAGES - START[b1]:
+                    nc.sync.dma_start(out=whole[:, part, :], in_=best[b1][:, part, :])
             feed(1)
 
         transpose_w(0)
@@ -314,27 +281,18 @@ def tile_nlgp_pa_kernel(tc, x, w_g, out):
         for b in range(1, X_AHEAD):
             regroup_x(b + 1)
             quantise_x(b)
-        feed_until("project", 0)
+        feed_until((project,), 0)
         quantise_g(0)
-        quantised.add(0)
         feed(1)
-        direct = [b for b in images if CHAIN[b] == 1]
         for s in images:
             if s + 1 < IMAGES:
-                feed_until("project", s + 1)
+                feed_until((project,), s + 1)
                 quantise_g(s + 1)
-                quantised.add(s + 1)
-                grams(count[0] + 0)
                 feed(1)
-                if s + 1 in NEGATED:
-                    negate_g(s + 1)
             if s + X_AHEAD + 1 < IMAGES:
                 regroup_x(s + X_AHEAD + 1)
-            if s + 1 in NEGATED:
-                quantise_negated(s + 1)
             if s + X_AHEAD < IMAGES:
                 quantise_x(s + X_AHEAD)
-                feed(0)
             for r in direct:
                 if r < s:
                     maximum(r, s)
@@ -343,5 +301,5 @@ def tile_nlgp_pa_kernel(tc, x, w_g, out):
         for group in ((3, 4, 5), (6, 7)):
             for b2 in images:
                 for r in group:
-                    if b2 >= CHAIN[r]:
+                    if b2 >= START[r]:
                         maximum(r, b2)

@@ -54,6 +54,14 @@ def tile_nlgp_pa_kernel(tc, x, w_g, out):
         w_scales = keep.tile([P, CHANNELS], U8, name="w_scales", align_bytes=64)
         identity = keep.tile([P, P], F32, name="identity")
 
+        idle = keep.tile([P, 512], BF16, name="idle")
+        nc.vector.memset(idle[:], 0.0)
+
+        def warm_up(count):
+            w_bank = psum_vector.tile([P, 512], F32, name="warm", tag="bank")
+            for n in range(count):
+                nc.tensor.matmul(w_bank[:], lhsT=idle[:, :P], rhs=idle[:], start=True, stop=True)
+
         def load_w(half):
             first_t = 2 * half
             nc.sync.dma_start(
@@ -94,13 +102,11 @@ def tile_nlgp_pa_kernel(tc, x, w_g, out):
         def transpose_w(half):
             w_words = w_raw[:].bitcast(F32).rearrange("p (t q u) -> p t u q", t=PACK, u=PAIR)
             grouped_words = w_grouped[:].bitcast(F32).rearrange("q (t p u) -> q t p u", t=PACK, u=PAIR)
-            w_bank = psum_scalar.tile([P, 2, PAIR, P], F32, name="w_bank", tag="bank")
-            for t in range(2):
+            for t in range(2 * half, 2 * half + 2):
+                w_bank = psum_scalar.tile([P, PAIR, P], F32, name="w_bank", tag="bank")
                 for u in range(PAIR):
-                    nc.tensor.transpose(w_bank[:, t, u, :], w_words[:, 2 * half + t, u, :], identity[:])
-            nc.scalar.copy(
-                out=grouped_words[:, 2 * half : 2 * half + 2, :, :], in_=w_bank[:].rearrange("q t u p -> q t p u")
-            )
+                    nc.tensor.transpose(w_bank[:, u, :], w_words[:, t, u, :], identity[:])
+                nc.scalar.copy(out=grouped_words[:, t, :, :], in_=w_bank[:].rearrange("q u p -> q p u"))
 
         def quantise_w(half):
             d_cols = slice(2 * half * P, (2 * half + 2) * P)
@@ -246,7 +252,20 @@ def tile_nlgp_pa_kernel(tc, x, w_g, out):
             while any([i[0] in kinds and i[1] == b for i in scalar_items]):
                 issue()
 
-        direct = [b for b in images if START[b] == 1]
+        early = range(3)
+        early_maxima = [[] for s in range(IMAGES + 1)]
+        for s in images:
+            late = []
+            for r in early:
+                if r < s and s >= START[r]:
+                    early_maxima[s].append((r, s))
+                if s in early and START[s] <= r + 1 <= s:
+                    if START[s] == 1:
+                        early_maxima[s].append((s, r + 1))
+                    else:
+                        late.append((s, r + 1))
+            early_maxima[s + 1] += late
+        early_maxima[IMAGES - 1] += early_maxima[IMAGES]
         done = [0] * IMAGES
         total = [0]
 
@@ -271,8 +290,10 @@ def tile_nlgp_pa_kernel(tc, x, w_g, out):
                     nc.sync.dma_start(out=whole[:, part, :], in_=best[b1][:, part, :])
             feed(1)
 
+        warm_up(5)
         transpose_w(0)
         transpose_w(1)
+        warm_up(2)
         regroup_x(0)
         quantise_w(0)
         quantise_x(0)
@@ -293,11 +314,8 @@ def tile_nlgp_pa_kernel(tc, x, w_g, out):
                 regroup_x(s + X_AHEAD + 1)
             if s + X_AHEAD < IMAGES:
                 quantise_x(s + X_AHEAD)
-            for r in direct:
-                if r < s:
-                    maximum(r, s)
-                    if s in direct:
-                        maximum(s, r + 1)
+            for r, b2 in early_maxima[s]:
+                maximum(r, b2)
         for group in ((3, 4, 5), (6, 7)):
             for b2 in images:
                 for r in group:

@@ -25,7 +25,7 @@ FLOPS = 2 * IMAGES * PIXELS * CHANNELS * (CHANNELS + IMAGES * PIXELS)
 SCALAR_BANKS = 4
 VECTOR_BANKS = 4
 RUN = 4
-START = (1, 1, 1, 3, 2, 2, 4, 5)
+START = (1, 2, 1, 3, 2, 2, 5, 5)
 X_AHEAD = 5
 SIGN = (1, -1) * (IMAGES // 2)
 
@@ -205,6 +205,8 @@ def tile_nlgp_pa_kernel(tc, x, w_g, out):
         def row_finish(b1):
             op = ALU.add if SIGN[b1] * SIGN[START[b1] - 1] > 0 else ALU.subtract
             nc.gpsimd.tensor_tensor(out=best[b1][:], in0=excess[b1][:], in1=base[b1][:], op=op)
+            if START[b1] == IMAGES:
+                nc.sync.dma_start(out=out.rearrange("(h p) b j -> p h b j", p=P)[:, :, b1, :], in_=best[b1][:])
 
         scalar_items = []
 
@@ -224,7 +226,7 @@ def tile_nlgp_pa_kernel(tc, x, w_g, out):
             return result
 
         rows = {b: segments(b) for b in images}
-        for word in "p0 p1 p2 r0 r1 p3 r2 p5 p4 r3 p7 p6 r3 r4 r5 r6 r7 r6 r7 r7 r6 r7".split(" "):
+        for word in "p0 p1 p2 p3 r0 r1 r2 p4 r3 p5 p6 r4 p7 r5 r6 r3 r7 r6 r7 r6 r7 r6 r7".split(" "):
             b = int(word[1:])
             if word[0] == "p":
                 scalar_items += [(project, b, h) for h in range(HALVES)]
@@ -241,7 +243,7 @@ def tile_nlgp_pa_kernel(tc, x, w_g, out):
                 return 0
             if item[0] == row_relu:
                 return 1
-            return 1.5 if item[0] in (row_step,) or (item[0] == row_first and START[item[1]] > 1) else 1
+            return 1 if item[0] in (row_step,) or (item[0] == row_first and START[item[1]] > 1) else 1
 
         def feed(count):
             credit[0] = min(credit[0] + count, 2)
@@ -288,7 +290,7 @@ def tile_nlgp_pa_kernel(tc, x, w_g, out):
                     )
                 if done[b1] == IMAGES - START[b1]:
                     nc.sync.dma_start(out=whole[:, part, :], in_=best[b1][:, part, :])
-            feed(1)
+            feed(.9)
 
         warm_up(5)
         transpose_w(0)
@@ -321,3 +323,5 @@ def tile_nlgp_pa_kernel(tc, x, w_g, out):
                 for r in group:
                     if b2 >= START[r]:
                         maximum(r, b2)
+        while scalar_items:
+            issue()

from contextlib import ExitStack

import concourse.mybir as mybir
from concourse.masks import make_identity

F32 = mybir.dt.float32
BF16 = mybir.dt.bfloat16
U32 = mybir.dt.uint32
U8 = mybir.dt.uint8
FP8X4 = mybir.dt.float8_e4m3fn_x4
ALU = mybir.AluOpType
COPY = mybir.ActivationFunctionType.Copy
RELU = mybir.ActivationFunctionType.Relu

P = 128
PACK = 4
IMAGES = 8
CHANNELS = 512
PIXELS = 256
HALVES = PIXELS // P
PAIR = 2

FLOPS = 2 * IMAGES * PIXELS * CHANNELS * (CHANNELS + IMAGES * PIXELS)

SCALAR_BANKS = 4
VECTOR_BANKS = 4
RUN = 4
START = (1, 2, 1, 3, 2, 2, 5, 5)
X_AHEAD = 5
SIGN = (1, -1) * (IMAGES // 2)


def tile_nlgp_pa_kernel(tc, x, w_g, out):
    nc = tc.nc
    with ExitStack() as ctx:
        keep = ctx.enter_context(tc.tile_pool(name="keep", bufs=1))
        work = ctx.enter_context(tc.tile_pool(name="work", bufs=4))
        psum_scalar = ctx.enter_context(tc.psum_pool(name="psum_scalar", bufs=SCALAR_BANKS))
        psum_vector = ctx.enter_context(tc.psum_pool(name="psum_vector", bufs=VECTOR_BANKS))
        ctx.enter_context(tc.manual_schedule())

        images = range(IMAGES)
        x_raw = [keep.tile([P, PACK, PIXELS], BF16, name="x_raw%d" % b) for b in images]
        x_grouped = [keep.tile([P, PIXELS, PACK], BF16, name="x_grouped%d" % b, align_bytes=64) for b in images]
        x_codes = [keep.tile([P, PIXELS], U32, name="x_codes%d" % b, align_bytes=64) for b in images]
        x_scales = [keep.tile([P, PIXELS], U8, name="x_scales%d" % b, align_bytes=64) for b in images]
        g_grouped = [keep.tile([P, PIXELS, PACK], BF16, name="g_grouped%d" % b, align_bytes=64) for b in images]
        g_codes = [keep.tile([P, PIXELS], U32, name="g_codes%d" % b, align_bytes=64) for b in images]
        g_scales = [keep.tile([P, PIXELS], U8, name="g_scales%d" % b, align_bytes=64) for b in images]
        best = [keep.tile([P, HALVES, PIXELS], F32, name="best%d" % b) for b in images]
        w_raw = keep.tile([P, PACK * CHANNELS], BF16, name="w_raw")
        w_grouped = keep.tile([P, CHANNELS * PACK], BF16, name="w_grouped", align_bytes=64)
        w_codes = keep.tile([P, CHANNELS], U32, name="w_codes", align_bytes=64)
        w_scales = keep.tile([P, CHANNELS], U8, name="w_scales", align_bytes=64)
        identity = keep.tile([P, P], F32, name="identity")

        idle = keep.tile([P, 512], BF16, name="idle")
        nc.vector.memset(idle[:], 0.0)

        def warm_up(count):
            w_bank = psum_vector.tile([P, 512], F32, name="warm", tag="bank")
            for n in range(count):
                nc.tensor.matmul(w_bank[:], lhsT=idle[:, :P], rhs=idle[:], start=True, stop=True)

        def load_w(half):
            first_t = 2 * half
            nc.sync.dma_start(
                out=w_raw[:, first_t * CHANNELS : (first_t + 2) * CHANNELS].rearrange("p (t c) -> p t c", t=2),
                in_=w_g.rearrange("(p t) c -> p t c", t=PACK)[:, first_t : first_t + 2, :],
            )

        def load_x(b):
            nc.sync.dma_start(out=x_raw[b][:], in_=x[b].rearrange("(q t) h w -> q t (h w)", t=PACK))

        load_w(0)
        load_w(1)
        load_x(0)
        load_x(1)
        load_x(2)
        load_x(3)
        load_x(4)
        load_x(5)
        load_x(6)
        load_x(7)
        make_identity(nc, identity[:])

        def regroup_x(b):
            target = x_grouped[b][:].rearrange("q (n i) t -> q n t i", i=RUN)
            source = x_raw[b][:].rearrange("q t (n i) -> q n t i", i=RUN)
            if b in ():
                nc.gpsimd.tensor_scalar(out=target, in0=source, scalar1=1.0, scalar2=0.0, op0=ALU.mult, op1=ALU.add)
            else:
                nc.vector.tensor_copy(out=target, in_=source)

        def quantise_x(b):
            nc.vector.quantize_mx(
                out=x_codes[b][:].bitcast(FP8X4),
                scales=x_scales[b][:],
                in_=x_grouped[b][:].rearrange("q i t -> q (i t)"),
            )

        def transpose_w(half):
            w_words = w_raw[:].bitcast(F32).rearrange("p (t q u) -> p t u q", t=PACK, u=PAIR)
            grouped_words = w_grouped[:].bitcast(F32).rearrange("q (t p u) -> q t p u", t=PACK, u=PAIR)
            for t in range(2 * half, 2 * half + 2):
                w_bank = psum_scalar.tile([P, PAIR, P], F32, name="w_bank", tag="bank")
                for u in range(PAIR):
                    nc.tensor.transpose(w_bank[:, u, :], w_words[:, t, u, :], identity[:])
                nc.scalar.copy(out=grouped_words[:, t, :, :], in_=w_bank[:].rearrange("q u p -> q p u"))

        def quantise_w(half):
            d_cols = slice(2 * half * P, (2 * half + 2) * P)
            nc.vector.quantize_mx(
                out=w_codes[:, d_cols].bitcast(FP8X4),
                scales=w_scales[:, d_cols],
                in_=w_grouped[:, 2 * half * P * PACK : (2 * half + 2) * P * PACK],
            )

        def project(b, h):
            pixels = slice(h * P, (h + 1) * P)
            g_bank = psum_scalar.tile([P, PACK, P], F32, name="g_bank", tag="bank")
            for t in range(PACK):
                d_cols = slice(t * P, (t + 1) * P)
                nc.tensor.matmul_mx(
                    out=g_bank[:, t, :],
                    lhsT=w_codes[:, d_cols].bitcast(FP8X4),
                    lhsT_scale=w_scales[:, d_cols],
                    rhs=x_codes[b][:, pixels].bitcast(FP8X4),
                    rhs_scale=x_scales[b][:, pixels],
                    start=True,
                    stop=True,
                )
            source = g_bank[:].rearrange("p t i -> p i t")
            if (b, h) in ():
                assert SIGN[b] > 0
                nc.vector.tensor_copy(out=g_grouped[b][:, pixels, :], in_=source)
            elif SIGN[b] > 0:
                nc.scalar.copy(out=g_grouped[b][:, pixels, :], in_=source)
            else:
                nc.scalar.activation(out=g_grouped[b][:, pixels, :], in_=source, func=COPY, scale=-1.0)

        def quantise_g(b):
            nc.vector.quantize_mx(
                out=g_codes[b][:].bitcast(FP8X4),
                scales=g_scales[b][:],
                in_=g_grouped[b][:].rearrange("p i t -> p (i t)"),
            )

        def gram(bank, b1, partners):
            for h in range(HALVES):
                rows = slice(h * P, (h + 1) * P)
                for n, b2 in enumerate(partners):
                    nc.tensor.matmul_mx(
                        out=bank[:, h, :],
                        lhsT=g_codes[b1][:, rows].bitcast(FP8X4),
                        lhsT_scale=g_scales[b1][:, rows],
                        rhs=g_codes[b2][:].bitcast(FP8X4),
                        rhs_scale=g_scales[b2][:],
                        start=(n == 0),
                        stop=(n == len(partners) - 1),
                    )

        def scalar_gram(b1, partners):
            p_bank = psum_scalar.tile([P, HALVES, PIXELS], F32, name="s_bank", tag="bank")
            gram(p_bank, b1, partners)
            return p_bank

        excess = {}
        shifted = {}
        base = {}

        def row_first(b1):
            if START[b1] == 1:
                p_bank = scalar_gram(b1, [0])
                if SIGN[b1] > 0:
                    nc.scalar.copy(out=best[b1][:], in_=p_bank[:])
                else:
                    nc.scalar.activation(out=best[b1][:], in_=p_bank[:], func=COPY, scale=-1.0)
                return
            p_bank = scalar_gram(b1, [0, 1])
            e = work.tile([P, HALVES, PIXELS], F32, name="e", tag="excess")
            nc.scalar.activation(out=e[:], in_=p_bank[:], func=RELU, scale=float(SIGN[b1]))
            excess[b1] = e

        def row_step(b1, n):
            p_bank = scalar_gram(b1, [n - 1, n])
            d = work.tile([P, HALVES, PIXELS], F32, name="d", tag="difference")
            nc.scalar.copy(out=d[:], in_=p_bank[:])
            s = work.tile([P, HALVES, PIXELS], F32, name="s", tag="shifted")
            op = ALU.add if SIGN[b1] * SIGN[n - 1] > 0 else ALU.subtract
            nc.gpsimd.tensor_tensor(out=s[:], in0=excess[b1][:], in1=d[:], op=op)
            shifted[b1] = s

        def row_relu(b1):
            e = work.tile([P, HALVES, PIXELS], F32, name="e", tag="excess")
            nc.scalar.activation(out=e[:], in_=shifted[b1][:], func=RELU)
            excess[b1] = e

        def row_base(b1):
            p_bank = scalar_gram(b1, [START[b1] - 1])
            c = work.tile([P, HALVES, PIXELS], F32, name="c", tag="base")
            nc.scalar.copy(out=c[:], in_=p_bank[:])
            base[b1] = c

        def row_finish(b1):
            op = ALU.add if SIGN[b1] * SIGN[START[b1] - 1] > 0 else ALU.subtract
            nc.gpsimd.tensor_tensor(out=best[b1][:], in0=excess[b1][:], in1=base[b1][:], op=op)
            if START[b1] == IMAGES:
                nc.sync.dma_start(out=out.rearrange("(h p) b j -> p h b j", p=P)[:, :, b1, :], in_=best[b1][:])

        scalar_items = []

        def segments(b):
            length = START[b]
            if length == 1:
                return [[(row_first, b)]]
            result = [[(row_first, b)]]
            for n in range(2, length):
                result[-1].append((row_step, b, n))
                result.append([(row_relu, b)])
            if length == 2:
                result[-1] += [(row_base, b), (row_finish, b)]
            else:
                result[-2].append((row_base, b)) if 0 else result[-1].insert(0, (row_base, b))
                result[-1].append((row_finish, b))
            return result

        rows = {b: segments(b) for b in images}
        for word in "p0 p1 p2 p3 r0 r1 r2 p4 r3 p5 p6 r4 p7 r5 r6 r3 r7 r6 r7 r6 r7 r6 r7".split(" "):
            b = int(word[1:])
            if word[0] == "p":
                scalar_items += [(project, b, h) for h in range(HALVES)]
            else:
                scalar_items += rows[b].pop(0)
        assert all([not r for r in rows.values()])

        credit = [0.0]

        def issue():
            item = scalar_items.pop(0)
            item[0](*item[1:])
            if item[0] == row_finish:
                return 0
            if item[0] == row_relu:
                return 1
            return 1 if item[0] in (row_step,) or (item[0] == row_first and START[item[1]] > 1) else 1

        def feed(count):
            credit[0] = min(credit[0] + count, 2)
            while credit[0] > 0 and scalar_items:
                credit[0] -= issue()

        def feed_until(kinds, b):
            while any([i[0] in kinds and i[1] == b for i in scalar_items]):
                issue()

        early = range(3)
        early_maxima = [[] for s in range(IMAGES + 1)]
        for s in images:
            late = []
            for r in early:
                if r < s and s >= START[r]:
                    early_maxima[s].append((r, s))
                if s in early and START[s] <= r + 1 <= s:
                    if START[s] == 1:
                        early_maxima[s].append((s, r + 1))
                    else:
                        late.append((s, r + 1))
            early_maxima[s + 1] += late
        early_maxima[IMAGES - 1] += early_maxima[IMAGES]
        done = [0] * IMAGES
        total = [0]

        def maximum(b1, b2):
            feed_until((row_first, row_finish), b1)
            p_bank = psum_vector.tile([P, HALVES, PIXELS], F32, name="p_bank", tag="bank")
            gram(p_bank, b1, [b2])
            total[0] += 1
            done[b1] += 1
            whole = out.rearrange("(h p) b j -> p h b j", p=P)[:, :, b1, :]
            parts = [slice(0, HALVES)]
            if total[0] == sum([IMAGES - n for n in START]):
                parts = [slice(h, h + 1) for h in range(HALVES)]
            for part in parts:
                if SIGN[b1] * SIGN[b2] > 0:
                    nc.vector.tensor_tensor(out=best[b1][:, part, :], in0=p_bank[:, part, :], in1=best[b1][:, part, :], op=ALU.max)
                else:
                    nc.vector.scalar_tensor_tensor(
                        out=best[b1][:, part, :], in0=p_bank[:, part, :], scalar=-1.0, in1=best[b1][:, part, :], op0=ALU.mult, op1=ALU.max
                    )
                if done[b1] == IMAGES - START[b1]:
                    nc.sync.dma_start(out=whole[:, part, :], in_=best[b1][:, part, :])
            feed(.9)

        warm_up(5)
        transpose_w(0)
        transpose_w(1)
        warm_up(2)
        regroup_x(0)
        quantise_w(0)
        quantise_x(0)
        quantise_w(1)
        regroup_x(1)
        for b in range(1, X_AHEAD):
            regroup_x(b + 1)
            quantise_x(b)
        feed_until((project,), 0)
        quantise_g(0)
        feed(1)
        for s in images:
            if s + 1 < IMAGES:
                feed_until((project,), s + 1)
                quantise_g(s + 1)
                feed(1)
            if s + X_AHEAD + 1 < IMAGES:
                regroup_x(s + X_AHEAD + 1)
            if s + X_AHEAD < IMAGES:
                quantise_x(s + X_AHEAD)
            for r, b2 in early_maxima[s]:
                maximum(r, b2)
        for group in ((3, 4, 5), (6, 7)):
            for b2 in images:
                for r in group:
                    if b2 >= START[r]:
                        maximum(r, b2)
        while scalar_items:
            issue()
